import numpy as np
import ml_dtypes


def mxq(x, axis, fmt="e4m3"):
    dtype, down = {"e4m3": (ml_dtypes.float8_e4m3fn, 7), "e5m2": (ml_dtypes.float8_e5m2, 14)}[fmt]
    v = np.moveaxis(np.asarray(x, np.float32).astype(ml_dtypes.bfloat16).astype(np.float64), axis, -1)
    blocks = v.reshape(v.shape[:-1] + (-1, 32))
    amax = np.abs(blocks).max(-1, keepdims=True)
    byte = np.maximum(np.where(amax > 0, np.frexp(amax)[1] - 1 + 127, 0) - down, 1)
    scale = np.exp2(byte - 127.0)
    codes = (blocks / scale).astype(np.float32).astype(dtype).astype(np.float64)
    return np.moveaxis((codes * scale).reshape(v.shape), -1, axis)


WIDE = False


def mx_kscale(k):
    if not WIDE:
        return np.ones(k)
    levels = np.array([10, -10, 5, -5, 0])
    if k % 512:
        return np.exp2(np.random.permutation(np.resize(levels, k // 32))).repeat(32)
    a = np.empty((k // 512, 16))
    for p in range(k // 512):
        a[p, :8] = np.random.permutation(np.resize(levels, 8))
        for g in range(8):
            far = levels[np.abs(levels - a[p, g]) >= 10]
            a[p, g + 8] = far[np.random.randint(len(far))]
    return np.exp2(a.ravel()).repeat(32)


BF16 = ml_dtypes.bfloat16


def bf(x):
    return np.asarray(x, np.float32).astype(BF16)


def f64(x):
    return np.asarray(x).astype(np.float64)


E2M1 = np.array([0.0, 0.5, 1.0, 1.5, 2.0, 3.0, 4.0, 6.0, -0.0, -0.5, -1.0, -1.5, -2.0, -3.0, -4.0, -6.0])


def pack_weight(w, fmt):
    k, n = w.shape
    w = f64(bf(w)).reshape(k // 32, 32, n)
    amax = np.abs(w).max(1)
    if fmt == "e4m3":
        byte = np.frexp(amax)[1] - 1 + 127 - 7
    else:
        mant, ex = np.frexp(amax / 6.0)
        byte = np.where(mant > 0.5, ex, ex - 1) + 127
    byte = np.clip(np.where(amax > 0, byte, 1), 1, 254)
    scaled = (w * np.exp2(127.0 - byte)[:, None, :]).reshape(k, n).astype(np.float32)
    by_word = np.ascontiguousarray(scaled.reshape(k // 512, 128, 4, n).transpose(0, 1, 3, 2))
    if fmt == "e4m3":
        words = by_word.astype(ml_dtypes.float8_e4m3fn).view(np.uint8)
    else:
        c = by_word.astype(ml_dtypes.float4_e2m1fn).view(np.uint8) & 0xF
        words = c[..., 0::2] | (c[..., 1::2] << 4)
    return np.ascontiguousarray(words), np.ascontiguousarray(byte.astype(np.uint8).reshape(k // 512, 16, n))


def unpack_weight(words, scales, fmt):
    g, p, n, _ = words.shape
    if fmt == "e4m3":
        vals = np.ascontiguousarray(words).view(ml_dtypes.float8_e4m3fn).astype(np.float64)
    else:
        nib = np.empty((g, p, n, 4), np.uint8)
        nib[..., 0::2] = words & 0xF
        nib[..., 1::2] = words >> 4
        vals = E2M1[nib]
    vals = vals * np.repeat(np.exp2(scales.astype(np.float64) - 127.0), 8, axis=1)[..., None]
    return vals.transpose(0, 1, 3, 2).reshape(g * 512, n)
def pack4(w):
    words, scales = pack_weight(w, "e2m1")
    return words.reshape(words.shape[0], 128, -1), scales


def unpack4(words, scales):
    return unpack_weight(words.reshape(words.shape[0], 128, -1, 2), scales, "e2m1")


B, N, D, H, S = 2, 512, 512, 1024, 128
QS = 2.3 / N ** 0.25


def silu(z):
    return z / (1.0 + np.exp(-z))


def draw0():
    t = np.exp2(np.round(np.log2(mx_kscale(N)) / 2))
    r = mx_kscale(H)
    q = bf(np.random.standard_normal((B, N, S)) * QS)
    k = bf(np.random.standard_normal((B, N, S)) * QS * t[:, None])
    u = bf(silu(0.7 * np.random.standard_normal((B, N, H))) * r)
    v = bf(silu(0.7 * np.random.standard_normal((B, N, H))) / (t * t)[:, None])
    W_o_words, W_o_scales = pack4(np.random.standard_normal((H, D)) / np.sqrt(H) / r[:, None])
    return {"q": q,
            "k": k,
            "u": u,
            "v": v,
            "W_o_words": W_o_words,
            "W_o_scales": W_o_scales,
            "b_o": bf(0.1 * np.random.standard_normal(D))}


def core(q, k, u, v, W_o_words, W_o_scales, b_o):
    qk = f64(q) @ f64(k).transpose(0, 2, 1) * (1.0 / np.sqrt(S))
    attn = np.square(np.maximum(qk, 0.0))
    av = mxq(attn, 2, "e4m3") @ mxq(f64(v), 1, "e4m3")
    gated = f64(u) * av
    return (mxq(gated, 2, "e4m3") @ unpack4(W_o_words, W_o_scales)) + f64(b_o)


def e4m3fn_bytes(y):
    return np.clip(np.asarray(y, np.float64), -448.0, 448.0).astype(np.float32).astype(ml_dtypes.float8_e4m3fn).view(np.uint8)


def e4m3fn_values(b):
    return np.asarray(b, np.uint8).view(ml_dtypes.float8_e4m3fn).astype(np.float64)


def setup_inputs():
    d = draw0()
    x0 = np.asarray(d['v']).astype(np.float64)
    s = (np.max(np.abs(x0), axis=(0, 2), keepdims=True) / 448.0).astype(np.float32)
    out = {}
    for k, v in d.items():
        if k == 'v':
            out['v_bytes'] = e4m3fn_bytes(x0 / s.astype(np.float64))
            out['v_scale'] = s
        else:
            out[k] = v
    return out


def reference(q, k, u, v_bytes, v_scale, W_o_words, W_o_scales, b_o):
    return core(q, k, u, e4m3fn_values(v_bytes) * v_scale.astype(np.float64), W_o_words, W_o_scales, b_o)

import math
from contextlib import ExitStack

import concourse.mybir as mybir
from concourse.masks import make_identity

B, N, D, H, S = 2, 512, 512, 1024, 128
FLOPS = B * (2 * N * N * S + 2 * N * N * H + 2 * N * H * D)

F32 = mybir.dt.float32
BF16 = mybir.dt.bfloat16
U32 = mybir.dt.uint32
I32 = mybir.dt.int32
U8 = mybir.dt.uint8
FP8 = mybir.dt.float8_e4m3fn
FP8X4 = mybir.dt.float8_e4m3fn_x4
FP4X4 = mybir.dt.float4_e2m1fn_x4
ACT = mybir.ActivationFunctionType
ALU = mybir.AluOpType

P = 128
T = 4
NT = N // P
G = H // 512
QK_SCALE = 1.0 / math.sqrt(S)

ORDER = """
SW00 VW01 PTq0 PTk0 VW02 SW03 VCQ0 PTU00 SCK0 VIL000 SIL010 VIL001 PQK00 VQV00 PTU01 SRL00 VW11 SSQ00 PQK01
VCU00 VQA00 SCU01 PQK02 VIL011 PAV000 SRL01 PTq1 VW13 SRL02 PQK03 VQV01 PTU02 SCQ1 SRL03 PAV001 VCU02 SSQ01
PTU03 VW12 PTk1 SCU03 VQA01 VGT000 SCK1 SSQ02 VGT001 PAV010 SSQ03 VGT010 PAV011 SW10 VQA02 VQG00 PAV020 VQA03
VGT011 SIL101 VGT020 PAV021 PPJ00 VIL111 PQK10 SIL100 VBI00 PQK11 PAV030 VQG01 PTU10 VGT021 PPJ01 SCU10 VGT030
PTU11 SIL110 VQV10 PAV031 PTU12 VQG02 VGT031 PPJ02 SRL10 VQV11 SSQ10 PQK12 VBI02 SRL11 VQG03 VQA10 SSQ11 VBI01
PAV100 SRL12 PAV101 VGT100 PPJ03 SSQ12 VGT101 PQK13 SRL13 VQG10 VBI03 PPJ10 SSQ13 VQA11 VQA12 SCU11 VQA13
PAV110 VBI10 PAV111 SCU12 PTU13 VGT110 VGT111 SCU13 PAV120 VQG11 PAV121 VGT120 PPJ11 VGT121 PAV130 VQG12
PAV131 VGT130 PPJ12 VGT131 VQY13 VBI12 VQX13 VBI11 PPX13 VBX13 PPY13 VBY13
"""


def tile_gatedattentionunit_pb_w4_kernel(tc, q, k, u, v_bytes, v_scale, W_o_words, W_o_scales, b_o, out):
    nc = tc.nc
    with ExitStack() as ctx:
        keep = ctx.enter_context(tc.tile_pool(name="keep", bufs=1))
        ps_tr = ctx.enter_context(tc.psum_pool(name="ps_tr", bufs=2))
        ps_qk = ctx.enter_context(tc.psum_pool(name="ps_qk", bufs=2))
        ps_av = ctx.enter_context(tc.psum_pool(name="ps_av", bufs=2))
        ps_o = ctx.enter_context(tc.psum_pool(name="ps_o", bufs=2))

        def kt(shape, dt, name):
            return keep.tile(shape, dt, name=name, align_bytes=64)

        k_sb = [kt([P, T, S], BF16, "k_sb%d" % b) for b in range(B)]
        q_sb = [kt([P, NT, S], BF16, "q_sb%d" % b) for b in range(B)]
        kT = [kt([P, T, P], BF16, "kT%d" % b) for b in range(B)]
        qT = [kt([P, NT, P], BF16, "qT%d" % b) for b in range(B)]
        vb = [kt([P, T, H], U8, "vb%d" % b) for b in range(B)]
        v_bf = [kt([P, T, H], BF16, "v_bf%d" % b) for b in range(B)]
        v_il = [[kt([P, T, P, T], BF16, "v_il%d_%d" % (b, g)) for g in range(G)] for b in range(B)]
        v_c = [[kt([P, 512], U32, "v_c%d_%d" % (b, g)) for g in range(G)] for b in range(B)]
        v_s = [[kt([P, 512], U8, "v_s%d_%d" % (b, g)) for g in range(G)] for b in range(B)]
        u_sb = [[kt([P, 2, H], BF16, "u_sb%d_%d" % (b, c)) for c in range(2)] for b in range(B)]
        uT = [[kt([P, G, P, T], BF16, "uT%d_%d" % (b, i)) for i in range(NT)] for b in range(B)]
        at_il = [[kt([P, P, T], BF16, "at_il%d_%d" % (b, i)) for i in range(NT)] for b in range(B)]
        at_c = [[kt([P, P], U32, "at_c%d_%d" % (b, i)) for i in range(NT)] for b in range(B)]
        at_s = [[kt([P, P], U8, "at_s%d_%d" % (b, i)) for i in range(NT)] for b in range(B)]
        r_sb = [[kt([P, P, T], F32, "r_sb%d_%d" % (b, i)) for i in range(NT)] for b in range(B)]
        gt = [[kt([P, G, P, T], BF16, "gt%d_%d" % (b, i)) for i in range(NT)] for b in range(B)]
        gc = [[kt([P, G, P], U32, "gc%d_%d" % (b, i)) for i in range(NT)] for b in range(B)]
        gs = [[kt([P, G, P], U8, "gs%d_%d" % (b, i)) for i in range(NT)] for b in range(B)]
        o_sb = [[kt([P, D], F32, "o_sb%d_%d" % (b, i)) for i in range(NT)] for b in range(B)]
        vs = kt([P, T], F32, "vs")
        w_sb = kt([P, G, 2 * D], U8, "w_sb")
        ws_sb = kt([P, G, D], U8, "ws_sb")
        b_bc = kt([P, D], BF16, "b_bc")
        id_bf = kt([P, P], BF16, "id_bf")
        id_f = kt([P, P], F32, "id_f")
        dummy = kt([P, 1], F32, "dummy")

        banks = {}

        def load_kq(b):
            nc.sync.dma_start(out=k_sb[b][:], in_=k[b].rearrange("(p t) s -> p t s", t=T))
            nc.sync.dma_start(out=q_sb[b][:], in_=q[b].rearrange("(p i) s -> p i s", i=NT))

        def load_v(b, t0, t1):
            rows = v_bytes[b].rearrange("(p t) h -> p t h", t=T)
            nc.sync.dma_start(out=vb[b][:, t0:t1, :], in_=rows[:, t0:t1, :])

        def load_u(b, c):
            rows = u[b].rearrange("(p i) h -> p i h", i=NT)
            nc.sync.dma_start(out=u_sb[b][c][:], in_=rows[:, 2 * c : 2 * c + 2, :])

        def load_w():
            nc.sync.dma_start(out=w_sb[:], in_=W_o_words.rearrange("g p n -> p g n"))
            rows = W_o_scales.bitcast(I32).rearrange("g (q r) n -> r q g n", r=4)
            ws_i = ws_sb[:].bitcast(I32)
            for r in range(4):
                nc.sync.dma_start(out=ws_i[r:P:32, :, :], in_=rows[r])
            nc.sync.dma_start(out=b_bc[:], in_=b_o.partition_broadcast(P))

        def copy(eng, out, in_):
            if eng == "V":
                nc.vector.tensor_copy(out=out, in_=in_)
            else:
                nc.scalar.copy(out=out, in_=in_)

        def Tk(e, b):
            bank = banks["Tk", b] = ps_tr.tile([P, T, P], BF16, name="tr_bank")
            for t in range(T):
                nc.tensor.transpose(bank[:, t, :], k_sb[b][:, t, :], id_bf[:])

        def Tq(e, b):
            bank = banks["Tq", b] = ps_tr.tile([P, T, P], BF16, name="tr_bank")
            for t in range(T):
                nc.tensor.transpose(bank[:, t, :], q_sb[b][:, t, :], id_bf[:])

        def CK(e, b):
            copy(e, kT[b][:], banks["Tk", b][:])

        def CQ(e, b):
            copy(e, qT[b][:], banks["Tq", b][:])

        def QK(e, b, i):
            bank = banks["QK", b, i] = ps_qk.tile([P, T, P], F32, name="qk_bank")
            for t in range(T):
                nc.tensor.matmul(bank[:, t, :], lhsT=kT[b][:, t, :], rhs=qT[b][:, i, :], start=True, stop=True)

        def RL(e, b, i):
            nc.scalar.activation(r_sb[b][i][:], banks["QK", b, i][:].rearrange("p t n -> p n t"), ACT.Relu)

        def SQ(e, b, i):
            nc.scalar.activation(at_il[b][i][:], r_sb[b][i][:], ACT.Square, scale=QK_SCALE)

        def QA(e, b, i):
            nc.vector.quantize_mx(out=at_c[b][i][:].bitcast(FP8X4), scales=at_s[b][i][:], in_=at_il[b][i][:].rearrange("p n t -> p (n t)"))

        def W(e, b, t):
            src = vb[b][:, t, :].bitcast(FP8)
            if e == "V":
                nc.vector.tensor_scalar(out=v_bf[b][:, t, :], in0=src, scalar1=vs[:, t : t + 1], scalar2=None, op0=ALU.mult)
            else:
                nc.scalar.activation(v_bf[b][:, t, :], src, ACT.Copy, scale=vs[:, t : t + 1])

        def IL(e, b, g, h):
            dst = v_il[b][g][:, 2 * h : 2 * h + 2]
            src = v_bf[b][:, :, 512 * g : 512 * (g + 1)].rearrange("p t (m c) -> p c m t", c=T)[:, 2 * h : 2 * h + 2]
            copy(e, dst, src)

        def QV(e, b, g):
            nc.vector.quantize_mx(out=v_c[b][g][:].bitcast(FP8X4), scales=v_s[b][g][:], in_=v_il[b][g][:].rearrange("p c m t -> p (c m t)"))

        def TU(e, b, i):
            bank = banks["TU", b, i] = ps_tr.tile([P, G, 2, P], F32, name="tr_bank")
            words = u_sb[b][i // 2][:, i % 2, :].bitcast(F32)
            for g in range(G):
                for w in range(2):
                    nc.tensor.transpose(bank[:, g, w, :], words[:, 256 * g + w : 256 * (g + 1) : 2], id_f[:])

        def CU(e, b, i):
            copy(e, uT[b][i][:].bitcast(F32), banks["TU", b, i][:].rearrange("p g w n -> p g n w"))

        def AV(e, b, i, g):
            bank = banks["AV", b, i, g] = ps_av.tile([P, T, P], F32, name="av_bank")
            for t in range(T):
                cols = slice(P * t, P * (t + 1))
                nc.tensor.matmul_mx(
                    out=bank[:, t, :],
                    lhsT=v_c[b][g][:, cols].bitcast(FP8X4),
                    lhsT_scale=v_s[b][g][:, cols],
                    rhs=at_c[b][i][:].bitcast(FP8X4),
                    rhs_scale=at_s[b][i][:],
                    start=True,
                    stop=True,
                )

        def GT(e, b, i, g):
            src = banks["AV", b, i, g][:].rearrange("p t n -> p n t")
            nc.vector.tensor_tensor(out=gt[b][i][:, g], in0=src, in1=uT[b][i][:, g], op=ALU.mult)

        def quant_gated(b, i, g0, g1):
            nc.vector.quantize_mx(
                out=gc[b][i][:, g0:g1].rearrange("p g n -> p (g n)").bitcast(FP8X4),
                scales=gs[b][i][:, g0:g1].rearrange("p g n -> p (g n)"),
                in_=gt[b][i][:, g0:g1].rearrange("p g n t -> p (g n t)"),
            )

        def QG(e, b, i):
            quant_gated(b, i, 0, G)

        def QX(e, b, i):
            quant_gated(b, i, 0, 1)

        def QY(e, b, i):
            quant_gated(b, i, 1, 2)

        def project(b, i, d0, d1, n):
            bank = banks["PJ", b, i, d0] = ps_o.tile([P, D], F32, name="o_bank")
            for c in range(d0, d1, n):
                for g in range(G):
                    nc.tensor.matmul_mx(
                        out=bank[:, c - d0 : c - d0 + n],
                        lhsT=gc[b][i][:, g, :].bitcast(FP8X4),
                        lhsT_scale=gs[b][i][:, g, :],
                        rhs=w_sb[:, g, 2 * c : 2 * (c + n)].bitcast(FP4X4),
                        rhs_scale=ws_sb[:, g, c : c + n],
                        start=(g == 0),
                        stop=(g == G - 1),
                    )

        def finish(b, i, d0, d1):
            o = o_sb[b][i][:, d0:d1]
            nc.vector.tensor_tensor(out=o, in0=banks["PJ", b, i, d0][:, : d1 - d0], in1=b_bc[:, d0:d1], op=ALU.add)
            nc.sync.dma_start(out=out[b].rearrange("(p i) d -> p i d", i=NT)[:, i, d0:d1], in_=o)

        def PJ(e, b, i):
            project(b, i, 0, D, D)

        def PX(e, b, i):
            project(b, i, 0, D // 2, 128)

        def PY(e, b, i):
            project(b, i, D // 2, D, 128)

        def BI(e, b, i):
            finish(b, i, 0, D)

        def BX(e, b, i):
            finish(b, i, 0, D // 2)

        def BY(e, b, i):
            finish(b, i, D // 2, D)

        make_identity(nc, id_bf[:])
        make_identity(nc, id_f[:])
        with tc.manual_schedule():
            nc.vector.memset(ws_sb[:].bitcast(I32), 0)
            nc.vector.memset(dummy[:], 0.0)
            nc.scalar.activation(dummy[:], dummy[:], ACT.Relu)

            nc.sync.dma_start(out=vs[:], in_=v_scale.rearrange("o (p t) x -> p (o t x)", t=T))
            load_v(0, 0, 1)
            load_v(0, 1, 2)
            load_kq(0)
            load_v(0, 2, 4)
            load_u(0, 0)
            load_u(0, 1)
            load_kq(1)
            load_v(1, 0, 2)
            load_v(1, 2, 4)
            load_w()
            load_u(1, 0)
            load_u(1, 1)
            table = dict(Tk=Tk, Tq=Tq, CK=CK, CQ=CQ, QK=QK, RL=RL, SQ=SQ, QA=QA, W=W, IL=IL, QV=QV, TU=TU, CU=CU, AV=AV, GT=GT, QG=QG, QX=QX, QY=QY, PJ=PJ, PX=PX, PY=PY, BI=BI, BX=BX, BY=BY)
            for step in ORDER.split():
                name = step[1 : 2 if step[1] == "W" else 3]
                table[name](step[0], *[int(c) for c in step[1 + len(name) :]])
